import numpy as np
import ml_dtypes


def mxq(x, axis, fmt="e4m3"):
    dtype, down = {"e4m3": (ml_dtypes.float8_e4m3fn, 7), "e5m2": (ml_dtypes.float8_e5m2, 14)}[fmt]
    v = np.moveaxis(np.asarray(x, np.float32).astype(ml_dtypes.bfloat16).astype(np.float64), axis, -1)
    blocks = v.reshape(v.shape[:-1] + (-1, 32))
    amax = np.abs(blocks).max(-1, keepdims=True)
    byte = np.maximum(np.where(amax > 0, np.frexp(amax)[1] - 1 + 127, 0) - down, 1)
    scale = np.exp2(byte - 127.0)
    codes = (blocks / scale).astype(np.float32).astype(dtype).astype(np.float64)
    return np.moveaxis((codes * scale).reshape(v.shape), -1, axis)


WIDE = False


def mx_kscale(k):
    if not WIDE:
        return np.ones(k)
    levels = np.array([10, -10, 5, -5, 0])
    a = np.random.permutation(np.resize(levels, k // 512 * 4)).reshape(k // 512, 4)
    idx = np.arange(k)
    return np.exp2(a[idx // 512, idx % 128 // 32])


BF16 = ml_dtypes.bfloat16


def bf(x):
    return np.asarray(x, np.float32).astype(BF16)


def f64(x):
    return np.asarray(x).astype(np.float64)


E2M1 = np.array([0.0, 0.5, 1.0, 1.5, 2.0, 3.0, 4.0, 6.0, -0.0, -0.5, -1.0, -1.5, -2.0, -3.0, -4.0, -6.0])


def pack_weight(w, fmt):
    k, n = w.shape
    w = f64(bf(w)).reshape(k // 32, 32, n)
    amax = np.abs(w).max(1)
    if fmt == "e4m3":
        byte = np.frexp(amax)[1] - 1 + 127 - 7
    else:
        mant, ex = np.frexp(amax / 6.0)
        byte = np.where(mant > 0.5, ex, ex - 1) + 127
    byte = np.clip(np.where(amax > 0, byte, 1), 1, 254)
    scaled = (w * np.exp2(127.0 - byte)[:, None, :]).reshape(k, n).astype(np.float32)
    by_word = np.ascontiguousarray(scaled.reshape(k // 512, 128, 4, n).transpose(0, 1, 3, 2))
    if fmt == "e4m3":
        words = by_word.astype(ml_dtypes.float8_e4m3fn).view(np.uint8)
    else:
        c = by_word.astype(ml_dtypes.float4_e2m1fn).view(np.uint8) & 0xF
        words = c[..., 0::2] | (c[..., 1::2] << 4)
    return np.ascontiguousarray(words), np.ascontiguousarray(byte.astype(np.uint8).reshape(k // 512, 16, n))


def unpack_weight(words, scales, fmt):
    g, p, n, _ = words.shape
    if fmt == "e4m3":
        vals = np.ascontiguousarray(words).view(ml_dtypes.float8_e4m3fn).astype(np.float64)
    else:
        nib = np.empty((g, p, n, 4), np.uint8)
        nib[..., 0::2] = words & 0xF
        nib[..., 1::2] = words >> 4
        vals = E2M1[nib]
    vals = vals * np.repeat(np.exp2(scales.astype(np.float64) - 127.0), 8, axis=1)[..., None]
    return vals.transpose(0, 1, 3, 2).reshape(g * 512, n)

def pack4(w):
    words, scales = pack_weight(w, "e2m1")
    return words.reshape(words.shape[0], 128, -1), scales


def unpack4(words, scales):
    return unpack_weight(words.reshape(words.shape[0], 128, -1, 2), scales, "e2m1")


B, DI, H = 2048, 512, 512
EPS = 1e-5


def _ln(v):
    m = np.mean(v, axis=-1, keepdims=True)
    var = np.var(v, axis=-1, keepdims=True)
    return (v - m) / np.sqrt(var + EPS)


def sigmoid(v):
    return 1.0 / (1.0 + np.exp(-v))


def setup_inputs():
    s = mx_kscale(DI)
    x = bf(np.random.standard_normal((B, DI)) * s)
    hx = bf(np.random.standard_normal((B, H)))
    w_i2h = np.random.standard_normal((3 * H, DI)) / np.sqrt(DI) / s[None, :]
    b_i2h = bf(np.random.standard_normal(3 * H) * 0.3)
    w_h2h = np.random.standard_normal((3 * H, H)) / np.sqrt(H)
    b_h2h = bf(np.random.standard_normal(3 * H) * 0.3)
    i_words, i_scales = pack4(np.ascontiguousarray(w_i2h.T))
    h_words, h_scales = pack4(np.ascontiguousarray(w_h2h.T))
    return {"x": x,
            "hx": hx,
            "W_i2h_words": i_words,
            "W_i2h_scales": i_scales,
            "b_i2h": b_i2h,
            "W_h2h_words": h_words,
            "W_h2h_scales": h_scales,
            "b_h2h": b_h2h}


def reference(x, hx, W_i2h_words, W_i2h_scales, b_i2h, W_h2h_words, W_h2h_scales, b_h2h):
    hx = f64(hx)
    xt = (mxq(f64(x), 1, "e4m3") @ unpack4(W_i2h_words, W_i2h_scales)) + f64(b_i2h)
    ht = (mxq(hx, 1, "e4m3") @ unpack4(W_h2h_words, W_h2h_scales)) + f64(b_h2h)
    x_new = xt[:, 2 * H:]
    h_new = ht[:, 2 * H:]
    gates = sigmoid(_ln(xt[:, : 2 * H]) + _ln(ht[:, : 2 * H]))
    r_t = gates[:, :H]
    z_t = gates[:, H:]
    n_t = np.tanh(_ln(x_new) + r_t * _ln(h_new))
    h_t = z_t * hx + (1.0 - z_t) * n_t
    return h_t

@@ -1,0 +1,231 @@
+from contextlib import ExitStack
+
+import concourse.mybir as mybir
+from concourse.masks import make_identity
+
+F32 = mybir.dt.float32
+BF16 = mybir.dt.bfloat16
+I32 = mybir.dt.int32
+U32 = mybir.dt.uint32
+U8 = mybir.dt.uint8
+FP8X4 = mybir.dt.float8_e4m3fn_x4
+FP4X4 = mybir.dt.float4_e2m1fn_x4
+ALU = mybir.AluOpType
+ACT = mybir.ActivationFunctionType
+AX = mybir.AxisListType
+
+P = 128
+B = 2048
+K = 512
+H = 512
+NT = B // P
+EPS = 1e-5
+FLOPS = 2 * B * K * 6 * H
+
+LAST_ON_VECTOR = 2
+V_BUFS = 8
+
+
+def tile_layernormgrucell_kernel(tc, x, hx, wi_words, wi_scales, b_i, wh_words, wh_scales, b_h, out):
+    nc = tc.nc
+    with ExitStack() as ctx:
+        const = ctx.enter_context(tc.tile_pool(name="const", bufs=1))
+        stage = ctx.enter_context(tc.tile_pool(name="stage", bufs=3))
+        work = ctx.enter_context(tc.tile_pool(name="work", bufs=V_BUFS))
+        small = ctx.enter_context(tc.tile_pool(name="small", bufs=V_BUFS))
+        ps_mm = ctx.enter_context(tc.psum_pool(name="ps_mm", bufs=6))
+        ps_tp = ctx.enter_context(tc.psum_pool(name="ps_tp", bufs=2))
+
+        w_planes = const.tile([P, 2, 3 * H], U8, align_bytes=64)
+        nc.vector.memset(w_planes[:].bitcast(I32), 0)
+        b_rows = const.tile([P, 6 * H], BF16)
+        nc.vector.memset(b_rows[:], 0.0)
+        ones = const.tile([P, P], BF16)
+        nc.vector.memset(ones[:], 1.0)
+        warm = const.tile([P, 1], F32)
+        nc.vector.memset(warm[:], 0.0)
+        nc.scalar.activation(out=warm[:], in_=warm[:], func=ACT.Sigmoid)
+        ident = const.tile([P, P], F32)
+        make_identity(nc, ident[:])
+
+        x_sb = const.tile([P, NT, K], BF16)
+        h_sb = const.tile([P, NT, K], BF16)
+        x_v = x.rearrange("(p t) k -> p t k", t=NT)
+        h_v = hx.rearrange("(p t) k -> p t k", t=NT)
+        out_v = out.rearrange("(p t) n -> p t n", t=NT)
+        w_words = const.tile([P, 2, 6 * H], U8, align_bytes=64)
+
+        def load_acts(t0, t1):
+            nc.sync.dma_start(out=x_sb[:, t0:t1, :], in_=x_v[:, t0:t1, :])
+            nc.sync.dma_start(out=h_sb[:, t0:t1, :], in_=h_v[:, t0:t1, :])
+
+        load_acts(0, 1)
+        nc.scalar.dma_start(out=b_rows[0:1, 0 : 3 * H], in_=b_i.unsqueeze(0))
+        nc.scalar.dma_start(out=b_rows[0:1, 3 * H : 6 * H], in_=b_h.unsqueeze(0))
+        for o, (words, scales) in enumerate(((wi_words, wi_scales), (wh_words, wh_scales))):
+            by_row = scales[0].bitcast(I32).rearrange("(q r) n -> r q n", r=4)
+            for r in range(4):
+                nc.sync.dma_start(out=w_planes[r:P:32, o, :].bitcast(I32), in_=by_row[r])
+            nc.sync.dma_start(out=w_words[:, o, :].bitcast(I32), in_=words[0].bitcast(I32))
+        load_acts(1, 2)
+        load_acts(2, 4)
+        load_acts(4, 8)
+        load_acts(8, 16)
+
+        k_mean = const.tile([P, 2, 4], F32)
+        nc.vector.memset(k_mean[:, 0, 0:2], -1.0 / (2 * H))
+        nc.vector.memset(k_mean[:, 0, 2:4], -1.0 / H)
+        nc.vector.memset(k_mean[:, 1, 0:2], -1.0 / (2 * H) / (2 * H) ** 0.5)
+        nc.vector.memset(k_mean[:, 1, 2:4], -1.0 / H / H**0.5)
+        eps_t = const.tile([P, 1], F32)
+        nc.vector.memset(eps_t[:], EPS)
+        m_half = const.tile([P, 4], F32)
+        nc.vector.memset(m_half[:], -0.5)
+
+        bias = const.tile([P, 6 * H], F32)
+        for j in range(6):
+            pb = ps_mm.tile([P, H], F32, tag="mm")
+            nc.tensor.matmul(out=pb[:], lhsT=ones[:], rhs=b_rows[:, j * H : (j + 1) * H], start=True, stop=True)
+            if j % 2 == 0:
+                nc.vector.tensor_copy(out=bias[:, j * H : (j + 1) * H], in_=pb[:])
+            else:
+                nc.scalar.copy(out=bias[:, j * H : (j + 1) * H], in_=pb[:])
+
+        acc_col = (4, 5, 2, 6, 7, 3)
+        st = {}
+
+        def transposes(t):
+            tp = ps_tp.tile([P, 4, P], F32, tag="tp")
+            for o, src in enumerate((x_sb, h_sb)):
+                for u in range(2):
+                    nc.tensor.transpose(tp[:, 2 * o + u, :], src[:].bitcast(F32)[:, t, u : K // 2 : 2], ident[:])
+            grouped = stage.tile([P, 2 * P * 4], BF16, align_bytes=64, tag="grouped")
+            nc.scalar.copy(
+                out=grouped[:].bitcast(F32).rearrange("p (o r u) -> p o r u", o=2, u=2),
+                in_=tp[:].rearrange("p (o u) r -> p o r u", o=2),
+            )
+            st[("grouped", t)] = grouped
+
+        def quantise(t):
+            a_words = stage.tile([P, 2 * P], U32, align_bytes=64, tag="a_words")
+            a_planes = stage.tile([P, 2 * P], U8, align_bytes=64, tag="a_planes")
+            nc.vector.quantize_mx(out=a_words[:].bitcast(FP8X4), scales=a_planes[:], in_=st[("grouped", t)][:])
+            st[("aq", t)] = (a_words, a_planes)
+
+        def project(t, j):
+            a_words, a_planes = st[("aq", t)]
+            o, c = divmod(j, 3)
+            pm = ps_mm.tile([P, H], F32, tag="mm")
+            nc.tensor.matmul_mx(
+                out=pm[:],
+                lhsT=a_words[:, o * P : (o + 1) * P].bitcast(FP8X4),
+                lhsT_scale=a_planes[:, o * P : (o + 1) * P],
+                rhs=w_words[:, o, c * 2 * H : (c + 1) * 2 * H].bitcast(FP4X4),
+                rhs_scale=w_planes[:, o, c * H : (c + 1) * H],
+                start=True,
+                stop=True,
+            )
+            st[("pm", t, j)] = pm
+
+        def add_bias(t, j):
+            if j == 0:
+                st[("v", t)] = work.tile([P, 6 * H], F32, tag="v", name="v")
+                st[("acc", t)] = small.tile([P, 8], F32, tag="acc", name="acc")
+            v, acc = st[("v", t)], st[("acc", t)]
+            nc.vector.scalar_tensor_tensor(
+                out=v[:, j * H : (j + 1) * H],
+                in0=st[("pm", t, j)][:],
+                scalar=0.0,
+                in1=bias[:, j * H : (j + 1) * H],
+                op0=ALU.add,
+                op1=ALU.add,
+                accum_out=acc[:, acc_col[j] : acc_col[j] + 1],
+            )
+
+        def means(t):
+            acc = st[("acc", t)]
+            nc.vector.tensor_reduce(
+                out=acc[:, 0:2], in_=acc[:, 4:8].rearrange("p (a b) -> p a b", b=2), axis=AX.X, op=ALU.add
+            )
+            nmb = small.tile([P, 2, 4], F32, tag="nmb")
+            nc.vector.tensor_tensor(
+                out=nmb[:], in0=acc[:, 0:4].unsqueeze(1).to_broadcast([P, 2, 4]), in1=k_mean[:], op=ALU.mult
+            )
+            st[("nmb", t)] = nmb
+
+        def variances(t):
+            v, nmb = st[("v", t)], st[("nmb", t)]
+            var = small.tile([P, 4], F32, tag="var")
+            junk = stage.tile([P, 2 * H], BF16, tag="junk")
+            parts = (v[:, 0 : 2 * H], v[:, 3 * H : 5 * H], v[:, 2 * H : 3 * H], v[:, 5 * H : 6 * H])
+            for col, part in enumerate(parts):
+                n_cols = part.shape[1]
+                nc.scalar.activation(
+                    out=junk[:, 0:n_cols],
+                    in_=part,
+                    func=ACT.Square,
+                    scale=1.0 / n_cols**0.5,
+                    bias=nmb[:, 1, col : col + 1],
+                    accum_out=var[:, col : col + 1],
+                )
+            ve = small.tile([P, 4], F32, tag="ve")
+            nc.scalar.activation(out=ve[:], in_=var[:], func=ACT.Identity, bias=eps_t[:, 0:1], scale=1.0)
+            rstd = small.tile([P, 4], F32, tag="rstd")
+            nc.gpsimd.tensor_tensor(out=rstd[:], in0=ve[:], in1=m_half[:], op=ALU.pow)
+            st[("ve", t)] = ve
+            st[("rstd", t)] = rstd
+
+        def gates(t):
+            v, nmb, ve, rstd = st[("v", t)], st[("nmb", t)], st[("ve", t)], st[("rstd", t)]
+            sd = small.tile([P, 2], F32, tag="sd")
+            nc.vector.tensor_tensor(out=sd[:], in0=ve[:, 0:4:2], in1=rstd[:, 0:4:2], op=ALU.mult)
+            rho = small.tile([P, 2], F32, tag="rho")
+            nc.vector.tensor_tensor(out=rho[:], in0=rstd[:, 1:4:2], in1=sd[:], op=ALU.mult)
+            mr = small.tile([P, 4], F32, tag="mr")
+            nc.vector.tensor_tensor(out=mr[:], in0=nmb[:, 0, :], in1=rstd[:], op=ALU.mult)
+            cg = small.tile([P, 1], F32, tag="cg")
+            nc.vector.tensor_tensor(out=cg[:], in0=mr[:, 0:1], in1=mr[:, 1:2], op=ALU.add)
+            xg, hg = v[:, 0 : 2 * H], v[:, 3 * H : 5 * H]
+            nc.vector.scalar_tensor_tensor(out=xg, in0=hg, scalar=rho[:, 0:1], in1=xg, op0=ALU.mult, op1=ALU.add)
+            nc.scalar.activation(out=xg, in_=xg, func=ACT.Sigmoid, scale=rstd[:, 0:1], bias=cg[:, 0:1])
+            st[("rho", t)] = rho
+            st[("mr", t)] = mr
+
+        def candidate(t):
+            v, nmb, rstd, rho, mr = st[("v", t)], st[("nmb", t)], st[("rstd", t)], st[("rho", t)], st[("mr", t)]
+            xn, hn, r_t = v[:, 2 * H : 3 * H], v[:, 5 * H : 6 * H], v[:, 0:H]
+            nc.vector.scalar_tensor_tensor(out=hn, in0=hn, scalar=nmb[:, 0, 3:4], in1=r_t, op0=ALU.add, op1=ALU.mult)
+            nc.vector.scalar_tensor_tensor(out=xn, in0=hn, scalar=rho[:, 1:2], in1=xn, op0=ALU.mult, op1=ALU.add)
+            nc.scalar.activation(out=xn, in_=xn, func=ACT.Tanh, scale=rstd[:, 2:3], bias=mr[:, 2:3])
+
+        def blend(t):
+            v = st[("v", t)]
+            eng = nc.gpsimd if t < NT - LAST_ON_VECTOR else nc.vector
+            xn, z_t, d, res = v[:, 2 * H : 3 * H], v[:, H : 2 * H], v[:, 3 * H : 4 * H], v[:, 4 * H : 5 * H]
+            eng.tensor_tensor(out=d, in0=h_sb[:, t, :], in1=xn, op=ALU.subtract)
+            eng.tensor_tensor(out=d, in0=z_t, in1=d, op=ALU.mult)
+            eng.tensor_tensor(out=res, in0=d, in1=xn, op=ALU.add)
+            nc.sync.dma_start(out=out_v[:, t, :], in_=res)
+
+        def live(t):
+            return 0 <= t < NT
+
+        with tc.manual_schedule():
+            for i in range(-3, NT + 4):
+                for j in range(6):
+                    if live(i):
+                        add_bias(i, j)
+                    if live(i + 1):
+                        project(i + 1, j)
+                if live(i):
+                    means(i)
+                    variances(i)
+                if live(i - 2):
+                    gates(i - 2)
+                if live(i - 3):
+                    candidate(i - 3)
+                    blend(i - 3)
+                if live(i + 3):
+                    transposes(i + 3)
+                if live(i + 2):
+                    quantise(i + 2)

@@ -22,7 +22,11 @@ NT = B // P
 EPS = 1e-5
 FLOPS = 2 * B * K * 6 * H
 
-LAST_ON_VECTOR = 2
+PE_E1 = True
+E3_GPSIMD_TILES = 0
+R_ON_GPSIMD = False
+OG, OC, OE = 2, 3, 4
+E2_POS = 2
 V_BUFS = 8
 
 
@@ -34,7 +38,8 @@ def tile_layernormgrucell_kernel(tc, x, hx, wi_words, wi_scales, b_i, wh_words, 
         work = ctx.enter_context(tc.tile_pool(name="work", bufs=V_BUFS))
         small = ctx.enter_context(tc.tile_pool(name="small", bufs=V_BUFS))
         ps_mm = ctx.enter_context(tc.psum_pool(name="ps_mm", bufs=6))
-        ps_tp = ctx.enter_context(tc.psum_pool(name="ps_tp", bufs=2))
+        ps_tp = ctx.enter_context(tc.psum_pool(name="ps_tp", bufs=1))
+        ps_d = ctx.enter_context(tc.psum_pool(name="ps_d", bufs=1))
 
         w_planes = const.tile([P, 2, 3 * H], U8, align_bytes=64)
         nc.vector.memset(w_planes[:].bitcast(I32), 0)
@@ -47,6 +52,8 @@ def tile_layernormgrucell_kernel(tc, x, hx, wi_words, wi_scales, b_i, wh_words, 
         nc.scalar.activation(out=warm[:], in_=warm[:], func=ACT.Sigmoid)
         ident = const.tile([P, P], F32)
         make_identity(nc, ident[:])
+        neg_ident = const.tile([P, P], BF16)
+        nc.vector.tensor_scalar(out=neg_ident[:], in0=ident[:], scalar1=-1.0, scalar2=None, op0=ALU.mult)
 
         x_sb = const.tile([P, NT, K], BF16)
         h_sb = const.tile([P, NT, K], BF16)
@@ -72,11 +79,9 @@ def tile_layernormgrucell_kernel(tc, x, hx, wi_words, wi_scales, b_i, wh_words, 
         load_acts(4, 8)
         load_acts(8, 16)
 
-        k_mean = const.tile([P, 2, 4], F32)
-        nc.vector.memset(k_mean[:, 0, 0:2], -1.0 / (2 * H))
-        nc.vector.memset(k_mean[:, 0, 2:4], -1.0 / H)
-        nc.vector.memset(k_mean[:, 1, 0:2], -1.0 / (2 * H) / (2 * H) ** 0.5)
-        nc.vector.memset(k_mean[:, 1, 2:4], -1.0 / H / H**0.5)
+        k_mean = const.tile([P, 4], F32)
+        nc.vector.memset(k_mean[:, 0:2], -1.0 / (2 * H))
+        nc.vector.memset(k_mean[:, 2:4], -1.0 / H)
         eps_t = const.tile([P, 1], F32)
         nc.vector.memset(eps_t[:], EPS)
         m_half = const.tile([P, 4], F32)
@@ -91,7 +96,7 @@ def tile_layernormgrucell_kernel(tc, x, hx, wi_words, wi_scales, b_i, wh_words, 
             else:
                 nc.scalar.copy(out=bias[:, j * H : (j + 1) * H], in_=pb[:])
 
-        acc_col = (4, 5, 2, 6, 7, 3)
+        banks = ((0, 0, 4), (0, 1, 5), (1, 0, 6), (1, 1, 7), (0, 2, 2), (1, 2, 3))
         st = {}
 
         def transposes(t):
@@ -114,7 +119,7 @@ def tile_layernormgrucell_kernel(tc, x, hx, wi_words, wi_scales, b_i, wh_words, 
 
         def project(t, j):
             a_words, a_planes = st[("aq", t)]
-            o, c = divmod(j, 3)
+            o, c = banks[j][0], banks[j][1]
             pm = ps_mm.tile([P, H], F32, tag="mm")
             nc.tensor.matmul_mx(
                 out=pm[:],
@@ -127,104 +132,121 @@ def tile_layernormgrucell_kernel(tc, x, hx, wi_words, wi_scales, b_i, wh_words, 
             )
             st[("pm", t, j)] = pm
 
+        def square(t, col, lo, n_cols):
+            v, acc, ss, junk = st[("v", t)], st[("acc", t)], st[("ss", t)], st[("junk", t)]
+            nc.scalar.activation(
+                out=junk[:, 0:n_cols],
+                in_=v[:, lo : lo + n_cols],
+                func=ACT.Square,
+                scale=-1.0 * n_cols,
+                bias=acc[:, col : col + 1],
+                accum_out=ss[:, col : col + 1],
+            )
+
         def add_bias(t, j):
             if j == 0:
                 st[("v", t)] = work.tile([P, 6 * H], F32, tag="v", name="v")
                 st[("acc", t)] = small.tile([P, 8], F32, tag="acc", name="acc")
+                st[("ss", t)] = small.tile([P, 4], F32, tag="ss", name="ss")
+                st[("junk", t)] = stage.tile([P, 2 * H], BF16, tag="junk", name="junk")
             v, acc = st[("v", t)], st[("acc", t)]
+            o, c, col = banks[j]
+            blk = 3 * o + c
             nc.vector.scalar_tensor_tensor(
-                out=v[:, j * H : (j + 1) * H],
+                out=v[:, blk * H : (blk + 1) * H],
                 in0=st[("pm", t, j)][:],
                 scalar=0.0,
-                in1=bias[:, j * H : (j + 1) * H],
+                in1=bias[:, blk * H : (blk + 1) * H],
                 op0=ALU.add,
                 op1=ALU.add,
-                accum_out=acc[:, acc_col[j] : acc_col[j] + 1],
+                accum_out=acc[:, col : col + 1],
             )
+            if j == 1 or j == 3:
+                nc.vector.tensor_reduce(out=acc[:, o : o + 1], in_=acc[:, col - 1 : col + 1], axis=AX.X, op=ALU.add)
+                square(t, o, 3 * o * H, 2 * H)
+            if j >= 4:
+                square(t, col, blk * H, H)
+            if j == 5:
+                rstds(t)
 
-        def means(t):
-            acc = st[("acc", t)]
-            nc.vector.tensor_reduce(
-                out=acc[:, 0:2], in_=acc[:, 4:8].rearrange("p (a b) -> p a b", b=2), axis=AX.X, op=ALU.add
-            )
-            nmb = small.tile([P, 2, 4], F32, tag="nmb")
-            nc.vector.tensor_tensor(
-                out=nmb[:], in0=acc[:, 0:4].unsqueeze(1).to_broadcast([P, 2, 4]), in1=k_mean[:], op=ALU.mult
-            )
-            st[("nmb", t)] = nmb
-
-        def variances(t):
-            v, nmb = st[("v", t)], st[("nmb", t)]
-            var = small.tile([P, 4], F32, tag="var")
-            junk = stage.tile([P, 2 * H], BF16, tag="junk")
-            parts = (v[:, 0 : 2 * H], v[:, 3 * H : 5 * H], v[:, 2 * H : 3 * H], v[:, 5 * H : 6 * H])
-            for col, part in enumerate(parts):
-                n_cols = part.shape[1]
-                nc.scalar.activation(
-                    out=junk[:, 0:n_cols],
-                    in_=part,
-                    func=ACT.Square,
-                    scale=1.0 / n_cols**0.5,
-                    bias=nmb[:, 1, col : col + 1],
-                    accum_out=var[:, col : col + 1],
-                )
+        def rstds(t):
+            ss = st[("ss", t)]
             ve = small.tile([P, 4], F32, tag="ve")
-            nc.scalar.activation(out=ve[:], in_=var[:], func=ACT.Identity, bias=eps_t[:, 0:1], scale=1.0)
+            nc.scalar.activation(
+                out=ve[:, 0:2], in_=ss[:, 0:2], func=ACT.Identity, bias=eps_t[:, 0:1], scale=1.0 / (2 * H) ** 3
+            )
+            nc.scalar.activation(out=ve[:, 2:4], in_=ss[:, 2:4], func=ACT.Identity, bias=eps_t[:, 0:1], scale=1.0 / H**3)
             rstd = small.tile([P, 4], F32, tag="rstd")
             nc.gpsimd.tensor_tensor(out=rstd[:], in0=ve[:], in1=m_half[:], op=ALU.pow)
             st[("ve", t)] = ve
             st[("rstd", t)] = rstd
+            if R_ON_GPSIMD:
+                row_scalars(t, nc.gpsimd)
+
+        def row_scalars(t, eng):
+            acc, ve, rstd = st[("acc", t)], st[("ve", t)], st[("rstd", t)]
+            nm = small.tile([P, 4], F32, tag="nm")
+            eng.tensor_tensor(out=nm[:], in0=acc[:, 0:4], in1=k_mean[:], op=ALU.mult)
+            sd = small.tile([P, 2], F32, tag="sd")
+            eng.tensor_tensor(out=sd[:], in0=ve[:, 0:4:2], in1=rstd[:, 0:4:2], op=ALU.mult)
+            rho = small.tile([P, 2], F32, tag="rho")
+            eng.tensor_tensor(out=rho[:], in0=rstd[:, 1:4:2], in1=sd[:], op=ALU.mult)
+            mr = small.tile([P, 4], F32, tag="mr")
+            eng.tensor_tensor(out=mr[:], in0=nm[:], in1=rstd[:], op=ALU.mult)
+            cg = small.tile([P, 1], F32, tag="cg")
+            eng.tensor_tensor(out=cg[:], in0=mr[:, 0:1], in1=mr[:, 1:2], op=ALU.add)
+            st[("rs", t)] = (nm, rho, mr, cg)
 
         def gates(t):
-            v, nmb, ve, rstd = st[("v", t)], st[("nmb", t)], st[("ve", t)], st[("rstd", t)]
-            sd = small.tile([P, 2], F32, tag="sd")
-            nc.vector.tensor_tensor(out=sd[:], in0=ve[:, 0:4:2], in1=rstd[:, 0:4:2], op=ALU.mult)
-            rho = small.tile([P, 2], F32, tag="rho")
-            nc.vector.tensor_tensor(out=rho[:], in0=rstd[:, 1:4:2], in1=sd[:], op=ALU.mult)
-            mr = small.tile([P, 4], F32, tag="mr")
-            nc.vector.tensor_tensor(out=mr[:], in0=nmb[:, 0, :], in1=rstd[:], op=ALU.mult)
-            cg = small.tile([P, 1], F32, tag="cg")
-            nc.vector.tensor_tensor(out=cg[:], in0=mr[:, 0:1], in1=mr[:, 1:2], op=ALU.add)
+            if not R_ON_GPSIMD:
+                row_scalars(t, nc.vector)
+            v, rstd = st[("v", t)], st[("rstd", t)]
+            nm, rho, mr, cg = st[("rs", t)]
             xg, hg = v[:, 0 : 2 * H], v[:, 3 * H : 5 * H]
             nc.vector.scalar_tensor_tensor(out=xg, in0=hg, scalar=rho[:, 0:1], in1=xg, op0=ALU.mult, op1=ALU.add)
             nc.scalar.activation(out=xg, in_=xg, func=ACT.Sigmoid, scale=rstd[:, 0:1], bias=cg[:, 0:1])
-            st[("rho", t)] = rho
-            st[("mr", t)] = mr
 
         def candidate(t):
-            v, nmb, rstd, rho, mr = st[("v", t)], st[("nmb", t)], st[("rstd", t)], st[("rho", t)], st[("mr", t)]
+            v, rstd = st[("v", t)], st[("rstd", t)]
+            nm, rho, mr, cg = st[("rs", t)]
             xn, hn, r_t = v[:, 2 * H : 3 * H], v[:, 5 * H : 6 * H], v[:, 0:H]
-            nc.vector.scalar_tensor_tensor(out=hn, in0=hn, scalar=nmb[:, 0, 3:4], in1=r_t, op0=ALU.add, op1=ALU.mult)
+            nc.vector.scalar_tensor_tensor(out=hn, in0=hn, scalar=nm[:, 3:4], in1=r_t, op0=ALU.add, op1=ALU.mult)
             nc.vector.scalar_tensor_tensor(out=xn, in0=hn, scalar=rho[:, 1:2], in1=xn, op0=ALU.mult, op1=ALU.add)
             nc.scalar.activation(out=xn, in_=xn, func=ACT.Tanh, scale=rstd[:, 2:3], bias=mr[:, 2:3])
+            if PE_E1:
+                pd = ps_d.tile([P, H], F32, tag="d")
+                nc.tensor.matmul(out=pd[:], lhsT=neg_ident[:], rhs=h_sb[:, t, :], start=True, stop=False)
+                nc.tensor.matmul(out=pd[:], lhsT=ident[:], rhs=xn, start=False, stop=True)
+                st[("pd", t)] = pd
 
         def blend(t):
             v = st[("v", t)]
-            eng = nc.gpsimd if t < NT - LAST_ON_VECTOR else nc.vector
             xn, z_t, d, res = v[:, 2 * H : 3 * H], v[:, H : 2 * H], v[:, 3 * H : 4 * H], v[:, 4 * H : 5 * H]
-            eng.tensor_tensor(out=d, in0=h_sb[:, t, :], in1=xn, op=ALU.subtract)
-            eng.tensor_tensor(out=d, in0=z_t, in1=d, op=ALU.mult)
-            eng.tensor_tensor(out=res, in0=d, in1=xn, op=ALU.add)
+            if PE_E1:
+                nc.vector.tensor_tensor(out=d, in0=st[("pd", t)][:], in1=z_t, op=ALU.mult)
+            else:
+                nc.vector.tensor_tensor(out=d, in0=xn, in1=h_sb[:, t, :], op=ALU.subtract)
+                nc.vector.tensor_tensor(out=d, in0=d, in1=z_t, op=ALU.mult)
+            eng = nc.gpsimd if t < E3_GPSIMD_TILES else nc.vector
+            eng.tensor_tensor(out=res, in0=xn, in1=d, op=ALU.subtract)
             nc.sync.dma_start(out=out_v[:, t, :], in_=res)
 
         def live(t):
             return 0 <= t < NT
 
         with tc.manual_schedule():
-            for i in range(-3, NT + 4):
+            for i in range(-3, NT + OE + 1):
                 for j in range(6):
+                    if j == E2_POS and live(i - OE):
+                        blend(i - OE)
                     if live(i):
                         add_bias(i, j)
                     if live(i + 1):
                         project(i + 1, j)
-                if live(i):
-                    means(i)
-                    variances(i)
-                if live(i - 2):
-                    gates(i - 2)
-                if live(i - 3):
-                    candidate(i - 3)
-                    blend(i - 3)
+                if live(i - OC):
+                    candidate(i - OC)
+                if live(i - OG):
+                    gates(i - OG)
                 if live(i + 3):
                     transposes(i + 3)
                 if live(i + 2):

@@ -22,11 +22,8 @@ NT = B // P
 EPS = 1e-5
 FLOPS = 2 * B * K * 6 * H
 
-PE_E1 = True
-E3_GPSIMD_TILES = 0
-R_ON_GPSIMD = False
-OG, OC, OE = 2, 3, 4
-E2_POS = 2
+OG, OC, OE = 1, 2, 3
+LAST_ON_VECTOR = 1
 V_BUFS = 8
 
 
@@ -52,7 +49,7 @@ def tile_layernormgrucell_kernel(tc, x, hx, wi_words, wi_scales, b_i, wh_words, 
         nc.scalar.activation(out=warm[:], in_=warm[:], func=ACT.Sigmoid)
         ident = const.tile([P, P], F32)
         make_identity(nc, ident[:])
-        neg_ident = const.tile([P, P], BF16)
+        neg_ident = const.tile([P, P], F32)
         nc.vector.tensor_scalar(out=neg_ident[:], in0=ident[:], scalar1=-1.0, scalar2=None, op0=ALU.mult)
 
         x_sb = const.tile([P, NT, K], BF16)
@@ -161,93 +158,164 @@ def tile_layernormgrucell_kernel(tc, x, hx, wi_words, wi_scales, b_i, wh_words, 
                 op1=ALU.add,
                 accum_out=acc[:, col : col + 1],
             )
-            if j == 1 or j == 3:
-                nc.vector.tensor_reduce(out=acc[:, o : o + 1], in_=acc[:, col - 1 : col + 1], axis=AX.X, op=ALU.add)
-                square(t, o, 3 * o * H, 2 * H)
-            if j >= 4:
-                square(t, col, blk * H, H)
-            if j == 5:
-                rstds(t)
+
+        def gate_sum(t, o):
+            acc = st[("acc", t)]
+            nc.vector.tensor_reduce(out=acc[:, o : o + 1], in_=acc[:, 4 + 2 * o : 6 + 2 * o], axis=AX.X, op=ALU.add)
+
+        def var_eps(t, half):
+            if half == 0:
+                st[("ve", t)] = small.tile([P, 4], F32, tag="ve", name="ve")
+            ss, ve = st[("ss", t)], st[("ve", t)]
+            n_cols = (2 * H, H)[half]
+            nc.scalar.activation(
+                out=ve[:, 2 * half : 2 * half + 2],
+                in_=ss[:, 2 * half : 2 * half + 2],
+                func=ACT.Identity,
+                bias=eps_t[:, 0:1],
+                scale=1.0 / n_cols**3,
+            )
 
         def rstds(t):
-            ss = st[("ss", t)]
-            ve = small.tile([P, 4], F32, tag="ve")
-            nc.scalar.activation(
-                out=ve[:, 0:2], in_=ss[:, 0:2], func=ACT.Identity, bias=eps_t[:, 0:1], scale=1.0 / (2 * H) ** 3
-            )
-            nc.scalar.activation(out=ve[:, 2:4], in_=ss[:, 2:4], func=ACT.Identity, bias=eps_t[:, 0:1], scale=1.0 / H**3)
             rstd = small.tile([P, 4], F32, tag="rstd")
-            nc.gpsimd.tensor_tensor(out=rstd[:], in0=ve[:], in1=m_half[:], op=ALU.pow)
-            st[("ve", t)] = ve
+            nc.gpsimd.tensor_tensor(out=rstd[:], in0=st[("ve", t)][:], in1=m_half[:], op=ALU.pow)
             st[("rstd", t)] = rstd
-            if R_ON_GPSIMD:
-                row_scalars(t, nc.gpsimd)
 
-        def row_scalars(t, eng):
-            acc, ve, rstd = st[("acc", t)], st[("ve", t)], st[("rstd", t)]
+        def rs_nm(t):
             nm = small.tile([P, 4], F32, tag="nm")
-            eng.tensor_tensor(out=nm[:], in0=acc[:, 0:4], in1=k_mean[:], op=ALU.mult)
+            nc.gpsimd.tensor_tensor(out=nm[:], in0=st[("acc", t)][:, 0:4], in1=k_mean[:], op=ALU.mult)
+            st[("nm", t)] = nm
+
+        def rs_sd(t):
             sd = small.tile([P, 2], F32, tag="sd")
-            eng.tensor_tensor(out=sd[:], in0=ve[:, 0:4:2], in1=rstd[:, 0:4:2], op=ALU.mult)
+            nc.gpsimd.tensor_tensor(out=sd[:], in0=st[("ve", t)][:, 0:4:2], in1=st[("rstd", t)][:, 0:4:2], op=ALU.mult)
+            st[("sd", t)] = sd
+
+        def rs_rho(t):
             rho = small.tile([P, 2], F32, tag="rho")
-            eng.tensor_tensor(out=rho[:], in0=rstd[:, 1:4:2], in1=sd[:], op=ALU.mult)
+            nc.gpsimd.tensor_tensor(out=rho[:], in0=st[("rstd", t)][:, 1:4:2], in1=st[("sd", t)][:], op=ALU.mult)
+            st[("rho", t)] = rho
+
+        def rs_mr(t):
             mr = small.tile([P, 4], F32, tag="mr")
-            eng.tensor_tensor(out=mr[:], in0=nm[:], in1=rstd[:], op=ALU.mult)
+            nc.gpsimd.tensor_tensor(out=mr[:], in0=st[("nm", t)][:], in1=st[("rstd", t)][:], op=ALU.mult)
+            st[("mr", t)] = mr
+
+        def rs_cg(t):
             cg = small.tile([P, 1], F32, tag="cg")
-            eng.tensor_tensor(out=cg[:], in0=mr[:, 0:1], in1=mr[:, 1:2], op=ALU.add)
-            st[("rs", t)] = (nm, rho, mr, cg)
+            mr = st[("mr", t)]
+            nc.gpsimd.tensor_tensor(out=cg[:], in0=mr[:, 0:1], in1=mr[:, 1:2], op=ALU.add)
+            st[("cg", t)] = cg
 
-        def gates(t):
-            if not R_ON_GPSIMD:
-                row_scalars(t, nc.vector)
-            v, rstd = st[("v", t)], st[("rstd", t)]
-            nm, rho, mr, cg = st[("rs", t)]
-            xg, hg = v[:, 0 : 2 * H], v[:, 3 * H : 5 * H]
-            nc.vector.scalar_tensor_tensor(out=xg, in0=hg, scalar=rho[:, 0:1], in1=xg, op0=ALU.mult, op1=ALU.add)
-            nc.scalar.activation(out=xg, in_=xg, func=ACT.Sigmoid, scale=rstd[:, 0:1], bias=cg[:, 0:1])
-
-        def candidate(t):
-            v, rstd = st[("v", t)], st[("rstd", t)]
-            nm, rho, mr, cg = st[("rs", t)]
-            xn, hn, r_t = v[:, 2 * H : 3 * H], v[:, 5 * H : 6 * H], v[:, 0:H]
-            nc.vector.scalar_tensor_tensor(out=hn, in0=hn, scalar=nm[:, 3:4], in1=r_t, op0=ALU.add, op1=ALU.mult)
-            nc.vector.scalar_tensor_tensor(out=xn, in0=hn, scalar=rho[:, 1:2], in1=xn, op0=ALU.mult, op1=ALU.add)
-            nc.scalar.activation(out=xn, in_=xn, func=ACT.Tanh, scale=rstd[:, 2:3], bias=mr[:, 2:3])
-            if PE_E1:
-                pd = ps_d.tile([P, H], F32, tag="d")
-                nc.tensor.matmul(out=pd[:], lhsT=neg_ident[:], rhs=h_sb[:, t, :], start=True, stop=False)
-                nc.tensor.matmul(out=pd[:], lhsT=ident[:], rhs=xn, start=False, stop=True)
-                st[("pd", t)] = pd
-
-        def blend(t):
+        def gates_sum(t):
             v = st[("v", t)]
-            xn, z_t, d, res = v[:, 2 * H : 3 * H], v[:, H : 2 * H], v[:, 3 * H : 4 * H], v[:, 4 * H : 5 * H]
-            if PE_E1:
-                nc.vector.tensor_tensor(out=d, in0=st[("pd", t)][:], in1=z_t, op=ALU.mult)
-            else:
-                nc.vector.tensor_tensor(out=d, in0=xn, in1=h_sb[:, t, :], op=ALU.subtract)
-                nc.vector.tensor_tensor(out=d, in0=d, in1=z_t, op=ALU.mult)
-            eng = nc.gpsimd if t < E3_GPSIMD_TILES else nc.vector
-            eng.tensor_tensor(out=res, in0=xn, in1=d, op=ALU.subtract)
+            xg, hg = v[:, 0 : 2 * H], v[:, 3 * H : 5 * H]
+            nc.vector.scalar_tensor_tensor(
+                out=xg, in0=hg, scalar=st[("rho", t)][:, 0:1], in1=xg, op0=ALU.mult, op1=ALU.add
+            )
+
+        def gates_act(t):
+            xg = st[("v", t)][:, 0 : 2 * H]
+            nc.scalar.activation(
+                out=xg, in_=xg, func=ACT.Sigmoid, scale=st[("rstd", t)][:, 0:1], bias=st[("cg", t)][:, 0:1]
+            )
+
+        def cand_reset(t):
+            v = st[("v", t)]
+            hn, r_t = v[:, 5 * H : 6 * H], v[:, 0:H]
+            nc.vector.scalar_tensor_tensor(
+                out=hn, in0=hn, scalar=st[("nm", t)][:, 3:4], in1=r_t, op0=ALU.add, op1=ALU.mult
+            )
+
+        def cand_sum(t):
+            v = st[("v", t)]
+            xn, hn = v[:, 2 * H : 3 * H], v[:, 5 * H : 6 * H]
+            nc.vector.scalar_tensor_tensor(
+                out=xn, in0=hn, scalar=st[("rho", t)][:, 1:2], in1=xn, op0=ALU.mult, op1=ALU.add
+            )
+
+        def cand_act(t):
+            xn = st[("v", t)][:, 2 * H : 3 * H]
+            nc.scalar.activation(
+                out=xn, in_=xn, func=ACT.Tanh, scale=st[("rstd", t)][:, 2:3], bias=st[("mr", t)][:, 2:3]
+            )
+
+        def blend_gpsimd(t):
+            v = st[("v", t)]
+            d = v[:, 3 * H : 4 * H]
+            nc.gpsimd.tensor_tensor(out=d, in0=v[:, 2 * H : 3 * H], in1=h_sb[:, t, :], op=ALU.subtract)
+            nc.gpsimd.tensor_tensor(out=d, in0=d, in1=v[:, H : 2 * H], op=ALU.mult)
+
+        def blend_out(t):
+            v = st[("v", t)]
+            po = ps_d.tile([P, H], F32, tag="d")
+            nc.tensor.matmul(out=po[:], lhsT=ident[:], rhs=v[:, 2 * H : 3 * H], start=True, stop=False)
+            nc.tensor.matmul(out=po[:], lhsT=neg_ident[:], rhs=v[:, 3 * H : 4 * H], start=False, stop=True)
+            st[("po", t)] = po
+
+        def store(t):
+            res = st[("v", t)][:, 4 * H : 5 * H]
+            nc.scalar.copy(out=res, in_=st[("po", t)][:])
+            nc.sync.dma_start(out=out_v[:, t, :], in_=res)
+
+        def blend_vector(t):
+            v = st[("v", t)]
+            d, res = v[:, 3 * H : 4 * H], v[:, 4 * H : 5 * H]
+            nc.vector.tensor_tensor(out=d, in0=v[:, 2 * H : 3 * H], in1=h_sb[:, t, :], op=ALU.subtract)
+            nc.vector.tensor_tensor(out=d, in0=d, in1=v[:, H : 2 * H], op=ALU.mult)
+            nc.vector.tensor_tensor(out=res, in0=v[:, 2 * H : 3 * H], in1=d, op=ALU.subtract)
             nc.sync.dma_start(out=out_v[:, t, :], in_=res)
 
         def live(t):
             return 0 <= t < NT
 
+        def at(t, fn, *args):
+            if live(t):
+                fn(t, *args)
+
+        def on_gpsimd(t):
+            return t < NT - LAST_ON_VECTOR
+
         with tc.manual_schedule():
-            for i in range(-3, NT + OE + 1):
-                for j in range(6):
-                    if j == E2_POS and live(i - OE):
-                        blend(i - OE)
-                    if live(i):
-                        add_bias(i, j)
-                    if live(i + 1):
-                        project(i + 1, j)
-                if live(i - OC):
-                    candidate(i - OC)
-                if live(i - OG):
-                    gates(i - OG)
-                if live(i + 3):
-                    transposes(i + 3)
-                if live(i + 2):
-                    quantise(i + 2)
+            for i in range(-2, NT + OE + 2):
+                if on_gpsimd(i - OE - 1):
+                    at(i - OE - 1, store)
+                if on_gpsimd(i - OE):
+                    at(i - OE, blend_gpsimd)
+                else:
+                    at(i - OE, blend_vector)
+                at(i + 2, transposes)
+                at(i, add_bias, 0)
+                at(i + 1, project, 0)
+                at(i, add_bias, 1)
+                at(i + 1, project, 1)
+                at(i, add_bias, 2)
+                at(i + 1, project, 2)
+                at(i, gate_sum, 0)
+                at(i, square, 0, 0, 2 * H)
+                at(i, add_bias, 3)
+                at(i + 1, project, 3)
+                at(i, add_bias, 4)
+                at(i + 1, project, 4)
+                at(i, gate_sum, 1)
+                at(i, square, 1, 3 * H, 2 * H)
+                at(i, square, 2, 2 * H, H)
+                at(i, var_eps, 0)
+                at(i, add_bias, 5)
+                at(i + 1, project, 5)
+                at(i, square, 3, 5 * H, H)
+                at(i, var_eps, 1)
+                at(i, rstds)
+                at(i, rs_sd)
+                at(i, rs_nm)
+                at(i, rs_rho)
+                at(i, rs_mr)
+                at(i, rs_cg)
+                at(i - OC, cand_reset)
+                at(i - OG, gates_sum)
+                at(i - OG, gates_act)
+                at(i + 2, quantise)
+                if on_gpsimd(i - OE):
+                    at(i - OE, blend_out)
+                at(i - OC, cand_sum)
+                at(i - OC, cand_act)

@@ -151,9 +151,9 @@ def tile_layernormgrucell_kernel(tc, x, hx, wi_words, wi_scales, b_i, wh_words, 
             blk = 3 * o + c
             nc.vector.scalar_tensor_tensor(
                 out=v[:, blk * H : (blk + 1) * H],
-                in0=st[("pm", t, j)][:],
+                in0=bias[:, blk * H : (blk + 1) * H],
                 scalar=0.0,
-                in1=bias[:, blk * H : (blk + 1) * H],
+                in1=st[("pm", t, j)][:],
                 op0=ALU.add,
                 op1=ALU.add,
                 accum_out=acc[:, col : col + 1],

@@ -38,15 +38,14 @@ def tile_layernormgrucell_kernel(tc, x, hx, wi_words, wi_scales, b_i, wh_words, 
         ps_tp = ctx.enter_context(tc.psum_pool(name="ps_tp", bufs=1))
         ps_d = ctx.enter_context(tc.psum_pool(name="ps_d", bufs=1))
 
-        w_planes = const.tile([P, 2, 3 * H], U8, align_bytes=64)
-        nc.vector.memset(w_planes[:].bitcast(I32), 0)
         b_rows = const.tile([P, 6 * H], BF16)
         nc.vector.memset(b_rows[:], 0.0)
+        w_planes = const.tile([P, 2, 3 * H], U8, align_bytes=64)
+        nc.vector.memset(w_planes[:].bitcast(I32), 0)
         ones = const.tile([P, P], BF16)
         nc.vector.memset(ones[:], 1.0)
         warm = const.tile([P, 1], F32)
         nc.vector.memset(warm[:], 0.0)
-        nc.scalar.activation(out=warm[:], in_=warm[:], func=ACT.Sigmoid)
         ident = const.tile([P, P], F32)
         make_identity(nc, ident[:])
         neg_ident = const.tile([P, P], F32)
@@ -66,6 +65,7 @@ def tile_layernormgrucell_kernel(tc, x, hx, wi_words, wi_scales, b_i, wh_words, 
         load_acts(0, 1)
         nc.scalar.dma_start(out=b_rows[0:1, 0 : 3 * H], in_=b_i.unsqueeze(0))
         nc.scalar.dma_start(out=b_rows[0:1, 3 * H : 6 * H], in_=b_h.unsqueeze(0))
+        nc.scalar.activation(out=warm[:], in_=warm[:], func=ACT.Sigmoid)
         for o, (words, scales) in enumerate(((wi_words, wi_scales), (wh_words, wh_scales))):
             by_row = scales[0].bitcast(I32).rearrange("(q r) n -> r q n", r=4)
             for r in range(4):
@@ -85,16 +85,15 @@ def tile_layernormgrucell_kernel(tc, x, hx, wi_words, wi_scales, b_i, wh_words, 
         nc.vector.memset(m_half[:], -0.5)
 
         bias = const.tile([P, 6 * H], F32)
-        for j in range(6):
-            pb = ps_mm.tile([P, H], F32, tag="mm")
-            nc.tensor.matmul(out=pb[:], lhsT=ones[:], rhs=b_rows[:, j * H : (j + 1) * H], start=True, stop=True)
-            if j % 2 == 0:
-                nc.vector.tensor_copy(out=bias[:, j * H : (j + 1) * H], in_=pb[:])
-            else:
-                nc.scalar.copy(out=bias[:, j * H : (j + 1) * H], in_=pb[:])
 
         banks = ((0, 0, 4), (0, 1, 5), (1, 0, 6), (1, 1, 7), (0, 2, 2), (1, 2, 3))
         st = {}
+
+        def spread_bias(j):
+            blk = 3 * banks[j][0] + banks[j][1]
+            pb = ps_mm.tile([P, H], F32, tag="mm")
+            nc.tensor.matmul(out=pb[:], lhsT=ones[:], rhs=b_rows[:, blk * H : (blk + 1) * H], start=True, stop=True)
+            nc.scalar.copy(out=bias[:, blk * H : (blk + 1) * H], in_=pb[:])
 
         def transposes(t):
             tp = ps_tp.tile([P, 4, P], F32, tag="tp")
@@ -183,28 +182,28 @@ def tile_layernormgrucell_kernel(tc, x, hx, wi_words, wi_scales, b_i, wh_words, 
 
         def rs_nm(t):
             nm = small.tile([P, 4], F32, tag="nm")
-            nc.gpsimd.tensor_tensor(out=nm[:], in0=st[("acc", t)][:, 0:4], in1=k_mean[:], op=ALU.mult)
+            nc.vector.tensor_tensor(out=nm[:], in0=st[("acc", t)][:, 0:4], in1=k_mean[:], op=ALU.mult)
             st[("nm", t)] = nm
 
         def rs_sd(t):
             sd = small.tile([P, 2], F32, tag="sd")
-            nc.gpsimd.tensor_tensor(out=sd[:], in0=st[("ve", t)][:, 0:4:2], in1=st[("rstd", t)][:, 0:4:2], op=ALU.mult)
+            nc.vector.tensor_tensor(out=sd[:], in0=st[("ve", t)][:, 0:4:2], in1=st[("rstd", t)][:, 0:4:2], op=ALU.mult)
             st[("sd", t)] = sd
 
         def rs_rho(t):
             rho = small.tile([P, 2], F32, tag="rho")
-            nc.gpsimd.tensor_tensor(out=rho[:], in0=st[("rstd", t)][:, 1:4:2], in1=st[("sd", t)][:], op=ALU.mult)
+            nc.vector.tensor_tensor(out=rho[:], in0=st[("rstd", t)][:, 1:4:2], in1=st[("sd", t)][:], op=ALU.mult)
             st[("rho", t)] = rho
 
         def rs_mr(t):
             mr = small.tile([P, 4], F32, tag="mr")
-            nc.gpsimd.tensor_tensor(out=mr[:], in0=st[("nm", t)][:], in1=st[("rstd", t)][:], op=ALU.mult)
+            nc.vector.tensor_tensor(out=mr[:], in0=st[("nm", t)][:], in1=st[("rstd", t)][:], op=ALU.mult)
             st[("mr", t)] = mr
 
         def rs_cg(t):
             cg = small.tile([P, 1], F32, tag="cg")
             mr = st[("mr", t)]
-            nc.gpsimd.tensor_tensor(out=cg[:], in0=mr[:, 0:1], in1=mr[:, 1:2], op=ALU.add)
+            nc.vector.tensor_tensor(out=cg[:], in0=mr[:, 0:1], in1=mr[:, 1:2], op=ALU.add)
             st[("cg", t)] = cg
 
         def gates_sum(t):
@@ -277,7 +276,18 @@ def tile_layernormgrucell_kernel(tc, x, hx, wi_words, wi_scales, b_i, wh_words, 
             return t < NT - LAST_ON_VECTOR
 
         with tc.manual_schedule():
-            for i in range(-2, NT + OE + 2):
+            transposes(0)
+            for j in range(3):
+                spread_bias(j)
+            quantise(0)
+            transposes(1)
+            for j in range(6):
+                project(0, j)
+                if j < 3:
+                    spread_bias(j + 3)
+            quantise(1)
+            for i in range(0, NT + OE + 2):
+                at(i - 1, rstds)
                 if on_gpsimd(i - OE - 1):
                     at(i - OE - 1, store)
                 if on_gpsimd(i - OE):
@@ -305,16 +315,15 @@ def tile_layernormgrucell_kernel(tc, x, hx, wi_words, wi_scales, b_i, wh_words, 
                 at(i + 1, project, 5)
                 at(i, square, 3, 5 * H, H)
                 at(i, var_eps, 1)
-                at(i, rstds)
-                at(i, rs_sd)
-                at(i, rs_nm)
-                at(i, rs_rho)
-                at(i, rs_mr)
-                at(i, rs_cg)
                 at(i - OC, cand_reset)
+                at(i - OG, rs_sd)
+                at(i - OG, rs_nm)
+                at(i - OG, rs_rho)
+                at(i - OG, rs_mr)
+                at(i + 2, quantise)
+                at(i - OG, rs_cg)
                 at(i - OG, gates_sum)
                 at(i - OG, gates_act)
-                at(i + 2, quantise)
                 if on_gpsimd(i - OE):
                     at(i - OE, blend_out)
                 at(i - OC, cand_sum)

@@ -100,10 +100,13 @@ def tile_layernormgrucell_kernel(tc, x, hx, wi_words, wi_scales, b_i, wh_words, 
             for o, src in enumerate((x_sb, h_sb)):
                 for u in range(2):
                     nc.tensor.transpose(tp[:, 2 * o + u, :], src[:].bitcast(F32)[:, t, u : K // 2 : 2], ident[:])
+            st[("tp", t)] = tp
+
+        def group(t):
             grouped = stage.tile([P, 2 * P * 4], BF16, align_bytes=64, tag="grouped")
             nc.scalar.copy(
                 out=grouped[:].bitcast(F32).rearrange("p (o r u) -> p o r u", o=2, u=2),
-                in_=tp[:].rearrange("p (o u) r -> p o r u", o=2),
+                in_=st[("tp", t)][:].rearrange("p (o u) r -> p o r u", o=2),
             )
             st[("grouped", t)] = grouped
 
@@ -131,7 +134,7 @@ def tile_layernormgrucell_kernel(tc, x, hx, wi_words, wi_scales, b_i, wh_words, 
         def square(t, col, lo, n_cols):
             v, acc, ss, junk = st[("v", t)], st[("acc", t)], st[("ss", t)], st[("junk", t)]
             nc.scalar.activation(
-                out=junk[:, 0:n_cols],
+                out=junk[:, lo : lo + n_cols],
                 in_=v[:, lo : lo + n_cols],
                 func=ACT.Square,
                 scale=-1.0 * n_cols,
@@ -144,7 +147,7 @@ def tile_layernormgrucell_kernel(tc, x, hx, wi_words, wi_scales, b_i, wh_words, 
                 st[("v", t)] = work.tile([P, 6 * H], F32, tag="v", name="v")
                 st[("acc", t)] = small.tile([P, 8], F32, tag="acc", name="acc")
                 st[("ss", t)] = small.tile([P, 4], F32, tag="ss", name="ss")
-                st[("junk", t)] = stage.tile([P, 2 * H], BF16, tag="junk", name="junk")
+                st[("junk", t)] = stage.tile([P, 6 * H], BF16, tag="junk", name="junk")
             v, acc = st[("v", t)], st[("acc", t)]
             o, c, col = banks[j]
             blk = 3 * o + c
@@ -277,24 +280,25 @@ def tile_layernormgrucell_kernel(tc, x, hx, wi_words, wi_scales, b_i, wh_words, 
 
         with tc.manual_schedule():
             transposes(0)
+            group(0)
             for j in range(3):
                 spread_bias(j)
             quantise(0)
             transposes(1)
+            group(1)
             for j in range(6):
                 project(0, j)
                 if j < 3:
                     spread_bias(j + 3)
             quantise(1)
+            transposes(2)
             for i in range(0, NT + OE + 2):
                 at(i - 1, rstds)
-                if on_gpsimd(i - OE - 1):
-                    at(i - OE - 1, store)
                 if on_gpsimd(i - OE):
                     at(i - OE, blend_gpsimd)
                 else:
                     at(i - OE, blend_vector)
-                at(i + 2, transposes)
+                at(i + 2, group)
                 at(i, add_bias, 0)
                 at(i + 1, project, 0)
                 at(i, add_bias, 1)
@@ -310,14 +314,17 @@ def tile_layernormgrucell_kernel(tc, x, hx, wi_words, wi_scales, b_i, wh_words, 
                 at(i, gate_sum, 1)
                 at(i, square, 1, 3 * H, 2 * H)
                 at(i, square, 2, 2 * H, H)
-                at(i, var_eps, 0)
                 at(i, add_bias, 5)
                 at(i + 1, project, 5)
+                at(i + 3, transposes)
                 at(i, square, 3, 5 * H, H)
+                if on_gpsimd(i - OE - 1):
+                    at(i - OE - 1, store)
+                at(i, var_eps, 0)
                 at(i, var_eps, 1)
-                at(i - OC, cand_reset)
                 at(i - OG, rs_sd)
                 at(i - OG, rs_nm)
+                at(i - OC, cand_reset)
                 at(i - OG, rs_rho)
                 at(i - OG, rs_mr)
                 at(i + 2, quantise)

@@ -328,10 +328,10 @@ def tile_layernormgrucell_kernel(tc, x, hx, wi_words, wi_scales, b_i, wh_words, 
                 at(i - OG, rs_rho)
                 at(i - OG, rs_mr)
                 at(i + 2, quantise)
+                at(i - OC, cand_sum)
+                at(i - OC, cand_act)
                 at(i - OG, rs_cg)
                 at(i - OG, gates_sum)
                 at(i - OG, gates_act)
                 if on_gpsimd(i - OE):
                     at(i - OE, blend_out)
-                at(i - OC, cand_sum)
-                at(i - OC, cand_act)

@@ -34,6 +34,7 @@ def tile_layernormgrucell_kernel(tc, x, hx, wi_words, wi_scales, b_i, wh_words, 
         stage = ctx.enter_context(tc.tile_pool(name="stage", bufs=3))
         work = ctx.enter_context(tc.tile_pool(name="work", bufs=V_BUFS))
         small = ctx.enter_context(tc.tile_pool(name="small", bufs=V_BUFS))
+        results = ctx.enter_context(tc.tile_pool(name="results", bufs=NT))
         ps_mm = ctx.enter_context(tc.psum_pool(name="ps_mm", bufs=6))
         ps_tp = ctx.enter_context(tc.psum_pool(name="ps_tp", bufs=1))
         ps_d = ctx.enter_context(tc.psum_pool(name="ps_d", bufs=1))
@@ -163,7 +164,10 @@ def tile_layernormgrucell_kernel(tc, x, hx, wi_words, wi_scales, b_i, wh_words, 
 
         def gate_sum(t, o):
             acc = st[("acc", t)]
-            nc.vector.tensor_reduce(out=acc[:, o : o + 1], in_=acc[:, 4 + 2 * o : 6 + 2 * o], axis=AX.X, op=ALU.add)
+            pair = small.tile([P, 2], F32, tag="pair", name="pair")
+            nc.scalar.activation(
+                out=pair[:], in_=acc[:, 4 + 2 * o : 6 + 2 * o], func=ACT.Identity, accum_out=acc[:, o : o + 1]
+            )
 
         def var_eps(t, half):
             if half == 0:
@@ -206,18 +210,18 @@ def tile_layernormgrucell_kernel(tc, x, hx, wi_words, wi_scales, b_i, wh_words, 
         def rs_cg(t):
             cg = small.tile([P, 1], F32, tag="cg")
             mr = st[("mr", t)]
-            nc.vector.tensor_tensor(out=cg[:], in0=mr[:, 0:1], in1=mr[:, 1:2], op=ALU.add)
+            nc.scalar.activation(out=cg[:], in_=mr[:, 0:1], func=ACT.Identity, bias=mr[:, 1:2])
             st[("cg", t)] = cg
 
-        def gates_sum(t):
+        def gates_sum(t, lo=0, hi=2 * H):
             v = st[("v", t)]
-            xg, hg = v[:, 0 : 2 * H], v[:, 3 * H : 5 * H]
+            xg, hg = v[:, lo:hi], v[:, 3 * H + lo : 3 * H + hi]
             nc.vector.scalar_tensor_tensor(
                 out=xg, in0=hg, scalar=st[("rho", t)][:, 0:1], in1=xg, op0=ALU.mult, op1=ALU.add
             )
 
-        def gates_act(t):
-            xg = st[("v", t)][:, 0 : 2 * H]
+        def gates_act(t, lo=0, hi=2 * H):
+            xg = st[("v", t)][:, lo:hi]
             nc.scalar.activation(
                 out=xg, in_=xg, func=ACT.Sigmoid, scale=st[("rstd", t)][:, 0:1], bias=st[("cg", t)][:, 0:1]
             )
@@ -256,17 +260,18 @@ def tile_layernormgrucell_kernel(tc, x, hx, wi_words, wi_scales, b_i, wh_words, 
             st[("po", t)] = po
 
         def store(t):
-            res = st[("v", t)][:, 4 * H : 5 * H]
-            nc.scalar.copy(out=res, in_=st[("po", t)][:])
-            nc.sync.dma_start(out=out_v[:, t, :], in_=res)
+            res = results.tile([P, H], F32, tag="res", name="res")
+            nc.scalar.copy(out=res[:], in_=st[("po", t)][:])
+            nc.sync.dma_start(out=out_v[:, t, :], in_=res[:])
 
         def blend_vector(t):
             v = st[("v", t)]
-            d, res = v[:, 3 * H : 4 * H], v[:, 4 * H : 5 * H]
+            d = v[:, 3 * H : 4 * H]
+            res = results.tile([P, H], F32, tag="res", name="res")
             nc.vector.tensor_tensor(out=d, in0=v[:, 2 * H : 3 * H], in1=h_sb[:, t, :], op=ALU.subtract)
             nc.vector.tensor_tensor(out=d, in0=d, in1=v[:, H : 2 * H], op=ALU.mult)
-            nc.vector.tensor_tensor(out=res, in0=v[:, 2 * H : 3 * H], in1=d, op=ALU.subtract)
-            nc.sync.dma_start(out=out_v[:, t, :], in_=res)
+            nc.vector.tensor_tensor(out=res[:], in0=v[:, 2 * H : 3 * H], in1=d, op=ALU.subtract)
+            nc.sync.dma_start(out=out_v[:, t, :], in_=res[:])
 
         def live(t):
             return 0 <= t < NT
@@ -298,22 +303,22 @@ def tile_layernormgrucell_kernel(tc, x, hx, wi_words, wi_scales, b_i, wh_words, 
                     at(i - OE, blend_gpsimd)
                 else:
                     at(i - OE, blend_vector)
-                at(i + 2, group)
                 at(i, add_bias, 0)
                 at(i + 1, project, 0)
                 at(i, add_bias, 1)
                 at(i + 1, project, 1)
+                at(i, gate_sum, 0)
+                at(i + 2, group)
                 at(i, add_bias, 2)
                 at(i + 1, project, 2)
-                at(i, gate_sum, 0)
                 at(i, square, 0, 0, 2 * H)
                 at(i, add_bias, 3)
                 at(i + 1, project, 3)
+                at(i, gate_sum, 1)
                 at(i, add_bias, 4)
                 at(i + 1, project, 4)
-                at(i, gate_sum, 1)
-                at(i, square, 1, 3 * H, 2 * H)
                 at(i, square, 2, 2 * H, H)
+                at(i, square, 1, 3 * H, 2 * H)
                 at(i, add_bias, 5)
                 at(i + 1, project, 5)
                 at(i + 3, transposes)
@@ -329,9 +334,14 @@ def tile_layernormgrucell_kernel(tc, x, hx, wi_words, wi_scales, b_i, wh_words, 
                 at(i - OG, rs_mr)
                 at(i + 2, quantise)
                 at(i - OC, cand_sum)
-                at(i - OC, cand_act)
                 at(i - OG, rs_cg)
-                at(i - OG, gates_sum)
-                at(i - OG, gates_act)
+                at(i - OC, cand_act)
+                if i - OG == NT - 1:
+                    for lo in (0, H):
+                        gates_sum(NT - 1, lo, lo + H)
+                        gates_act(NT - 1, lo, lo + H)
+                else:
+                    at(i - OG, gates_sum)
+                    at(i - OG, gates_act)
                 if on_gpsimd(i - OE):
                     at(i - OE, blend_out)

from contextlib import ExitStack

import concourse.mybir as mybir
from concourse.masks import make_identity

F32 = mybir.dt.float32
BF16 = mybir.dt.bfloat16
I32 = mybir.dt.int32
U32 = mybir.dt.uint32
U8 = mybir.dt.uint8
FP8X4 = mybir.dt.float8_e4m3fn_x4
FP4X4 = mybir.dt.float4_e2m1fn_x4
ALU = mybir.AluOpType
ACT = mybir.ActivationFunctionType
AX = mybir.AxisListType

P = 128
B = 2048
K = 512
H = 512
NT = B // P
EPS = 1e-5
FLOPS = 2 * B * K * 6 * H

OG, OC, OE = 1, 2, 3
LAST_ON_VECTOR = 1
V_BUFS = 8


def tile_layernormgrucell_kernel(tc, x, hx, wi_words, wi_scales, b_i, wh_words, wh_scales, b_h, out):
    nc = tc.nc
    with ExitStack() as ctx:
        const = ctx.enter_context(tc.tile_pool(name="const", bufs=1))
        stage = ctx.enter_context(tc.tile_pool(name="stage", bufs=3))
        work = ctx.enter_context(tc.tile_pool(name="work", bufs=V_BUFS))
        small = ctx.enter_context(tc.tile_pool(name="small", bufs=V_BUFS))
        results = ctx.enter_context(tc.tile_pool(name="results", bufs=NT))
        ps_mm = ctx.enter_context(tc.psum_pool(name="ps_mm", bufs=6))
        ps_tp = ctx.enter_context(tc.psum_pool(name="ps_tp", bufs=1))
        ps_d = ctx.enter_context(tc.psum_pool(name="ps_d", bufs=1))

        b_rows = const.tile([P, 6 * H], BF16)
        nc.vector.memset(b_rows[:], 0.0)
        w_planes = const.tile([P, 2, 3 * H], U8, align_bytes=64)
        nc.vector.memset(w_planes[:].bitcast(I32), 0)
        ones = const.tile([P, P], BF16)
        nc.vector.memset(ones[:], 1.0)
        warm = const.tile([P, 1], F32)
        nc.vector.memset(warm[:], 0.0)
        ident = const.tile([P, P], F32)
        make_identity(nc, ident[:])
        neg_ident = const.tile([P, P], F32)
        nc.vector.tensor_scalar(out=neg_ident[:], in0=ident[:], scalar1=-1.0, scalar2=None, op0=ALU.mult)

        x_sb = const.tile([P, NT, K], BF16)
        h_sb = const.tile([P, NT, K], BF16)
        x_v = x.rearrange("(p t) k -> p t k", t=NT)
        h_v = hx.rearrange("(p t) k -> p t k", t=NT)
        out_v = out.rearrange("(p t) n -> p t n", t=NT)
        w_words = const.tile([P, 2, 6 * H], U8, align_bytes=64)

        def load_acts(t0, t1):
            nc.sync.dma_start(out=x_sb[:, t0:t1, :], in_=x_v[:, t0:t1, :])
            nc.sync.dma_start(out=h_sb[:, t0:t1, :], in_=h_v[:, t0:t1, :])

        load_acts(0, 1)
        nc.scalar.dma_start(out=b_rows[0:1, 0 : 3 * H], in_=b_i.unsqueeze(0))
        nc.scalar.dma_start(out=b_rows[0:1, 3 * H : 6 * H], in_=b_h.unsqueeze(0))
        nc.scalar.activation(out=warm[:], in_=warm[:], func=ACT.Sigmoid)
        for o, (words, scales) in enumerate(((wi_words, wi_scales), (wh_words, wh_scales))):
            by_row = scales[0].bitcast(I32).rearrange("(q r) n -> r q n", r=4)
            for r in range(4):
                nc.sync.dma_start(out=w_planes[r:P:32, o, :].bitcast(I32), in_=by_row[r])
            nc.sync.dma_start(out=w_words[:, o, :].bitcast(I32), in_=words[0].bitcast(I32))
        load_acts(1, 2)
        load_acts(2, 4)
        load_acts(4, 8)
        load_acts(8, 16)

        k_mean = const.tile([P, 4], F32)
        nc.vector.memset(k_mean[:, 0:2], -1.0 / (2 * H))
        nc.vector.memset(k_mean[:, 2:4], -1.0 / H)
        eps_t = const.tile([P, 1], F32)
        nc.vector.memset(eps_t[:], EPS)
        m_half = const.tile([P, 4], F32)
        nc.vector.memset(m_half[:], -0.5)

        bias = const.tile([P, 6 * H], F32)

        banks = ((0, 0, 4), (0, 1, 5), (1, 0, 6), (1, 1, 7), (0, 2, 2), (1, 2, 3))
        st = {}

        def spread_bias(j):
            blk = 3 * banks[j][0] + banks[j][1]
            pb = ps_mm.tile([P, H], F32, tag="mm")
            nc.tensor.matmul(out=pb[:], lhsT=ones[:], rhs=b_rows[:, blk * H : (blk + 1) * H], start=True, stop=True)
            nc.scalar.copy(out=bias[:, blk * H : (blk + 1) * H], in_=pb[:])

        def transposes(t):
            tp = ps_tp.tile([P, 4, P], F32, tag="tp")
            for o, src in enumerate((x_sb, h_sb)):
                for u in range(2):
                    nc.tensor.transpose(tp[:, 2 * o + u, :], src[:].bitcast(F32)[:, t, u : K // 2 : 2], ident[:])
            st[("tp", t)] = tp

        def group(t):
            grouped = stage.tile([P, 2 * P * 4], BF16, align_bytes=64, tag="grouped")
            nc.scalar.copy(
                out=grouped[:].bitcast(F32).rearrange("p (o r u) -> p o r u", o=2, u=2),
                in_=st[("tp", t)][:].rearrange("p (o u) r -> p o r u", o=2),
            )
            st[("grouped", t)] = grouped

        def quantise(t):
            a_words = stage.tile([P, 2 * P], U32, align_bytes=64, tag="a_words")
            a_planes = stage.tile([P, 2 * P], U8, align_bytes=64, tag="a_planes")
            nc.vector.quantize_mx(out=a_words[:].bitcast(FP8X4), scales=a_planes[:], in_=st[("grouped", t)][:])
            st[("aq", t)] = (a_words, a_planes)

        def project(t, j):
            a_words, a_planes = st[("aq", t)]
            o, c = banks[j][0], banks[j][1]
            pm = ps_mm.tile([P, H], F32, tag="mm")
            nc.tensor.matmul_mx(
                out=pm[:],
                lhsT=a_words[:, o * P : (o + 1) * P].bitcast(FP8X4),
                lhsT_scale=a_planes[:, o * P : (o + 1) * P],
                rhs=w_words[:, o, c * 2 * H : (c + 1) * 2 * H].bitcast(FP4X4),
                rhs_scale=w_planes[:, o, c * H : (c + 1) * H],
                start=True,
                stop=True,
            )
            st[("pm", t, j)] = pm

        def square(t, col, lo, n_cols):
            v, acc, ss, junk = st[("v", t)], st[("acc", t)], st[("ss", t)], st[("junk", t)]
            nc.scalar.activation(
                out=junk[:, lo : lo + n_cols],
                in_=v[:, lo : lo + n_cols],
                func=ACT.Square,
                scale=-1.0 * n_cols,
                bias=acc[:, col : col + 1],
                accum_out=ss[:, col : col + 1],
            )

        def add_bias(t, j):
            if j == 0:
                st[("v", t)] = work.tile([P, 6 * H], F32, tag="v", name="v")
                st[("acc", t)] = small.tile([P, 8], F32, tag="acc", name="acc")
                st[("ss", t)] = small.tile([P, 4], F32, tag="ss", name="ss")
                st[("junk", t)] = stage.tile([P, 6 * H], BF16, tag="junk", name="junk")
            v, acc = st[("v", t)], st[("acc", t)]
            o, c, col = banks[j]
            blk = 3 * o + c
            nc.vector.scalar_tensor_tensor(
                out=v[:, blk * H : (blk + 1) * H],
                in0=bias[:, blk * H : (blk + 1) * H],
                scalar=0.0,
                in1=st[("pm", t, j)][:],
                op0=ALU.add,
                op1=ALU.add,
                accum_out=acc[:, col : col + 1],
            )

        def gate_sum(t, o):
            acc = st[("acc", t)]
            pair = small.tile([P, 2], F32, tag="pair", name="pair")
            nc.scalar.activation(
                out=pair[:], in_=acc[:, 4 + 2 * o : 6 + 2 * o], func=ACT.Identity, accum_out=acc[:, o : o + 1]
            )

        def var_eps(t, half):
            if half == 0:
                st[("ve", t)] = small.tile([P, 4], F32, tag="ve", name="ve")
            ss, ve = st[("ss", t)], st[("ve", t)]
            n_cols = (2 * H, H)[half]
            nc.scalar.activation(
                out=ve[:, 2 * half : 2 * half + 2],
                in_=ss[:, 2 * half : 2 * half + 2],
                func=ACT.Identity,
                bias=eps_t[:, 0:1],
                scale=1.0 / n_cols**3,
            )

        def rstds(t):
            rstd = small.tile([P, 4], F32, tag="rstd")
            nc.gpsimd.tensor_tensor(out=rstd[:], in0=st[("ve", t)][:], in1=m_half[:], op=ALU.pow)
            st[("rstd", t)] = rstd

        def rs_nm(t):
            nm = small.tile([P, 4], F32, tag="nm")
            nc.vector.tensor_tensor(out=nm[:], in0=st[("acc", t)][:, 0:4], in1=k_mean[:], op=ALU.mult)
            st[("nm", t)] = nm

        def rs_sd(t):
            sd = small.tile([P, 2], F32, tag="sd")
            nc.vector.tensor_tensor(out=sd[:], in0=st[("ve", t)][:, 0:4:2], in1=st[("rstd", t)][:, 0:4:2], op=ALU.mult)
            st[("sd", t)] = sd

        def rs_rho(t):
            rho = small.tile([P, 2], F32, tag="rho")
            nc.vector.tensor_tensor(out=rho[:], in0=st[("rstd", t)][:, 1:4:2], in1=st[("sd", t)][:], op=ALU.mult)
            st[("rho", t)] = rho

        def rs_mr(t):
            mr = small.tile([P, 4], F32, tag="mr")
            nc.vector.tensor_tensor(out=mr[:], in0=st[("nm", t)][:], in1=st[("rstd", t)][:], op=ALU.mult)
            st[("mr", t)] = mr

        def rs_cg(t):
            cg = small.tile([P, 1], F32, tag="cg")
            mr = st[("mr", t)]
            nc.scalar.activation(out=cg[:], in_=mr[:, 0:1], func=ACT.Identity, bias=mr[:, 1:2])
            st[("cg", t)] = cg

        def gates_sum(t, lo=0, hi=2 * H):
            v = st[("v", t)]
            xg, hg = v[:, lo:hi], v[:, 3 * H + lo : 3 * H + hi]
            nc.vector.scalar_tensor_tensor(
                out=xg, in0=hg, scalar=st[("rho", t)][:, 0:1], in1=xg, op0=ALU.mult, op1=ALU.add
            )

        def gates_act(t, lo=0, hi=2 * H):
            xg = st[("v", t)][:, lo:hi]
            nc.scalar.activation(
                out=xg, in_=xg, func=ACT.Sigmoid, scale=st[("rstd", t)][:, 0:1], bias=st[("cg", t)][:, 0:1]
            )

        def cand_reset(t):
            v = st[("v", t)]
            hn, r_t = v[:, 5 * H : 6 * H], v[:, 0:H]
            nc.vector.scalar_tensor_tensor(
                out=hn, in0=hn, scalar=st[("nm", t)][:, 3:4], in1=r_t, op0=ALU.add, op1=ALU.mult
            )

        def cand_sum(t):
            v = st[("v", t)]
            xn, hn = v[:, 2 * H : 3 * H], v[:, 5 * H : 6 * H]
            nc.vector.scalar_tensor_tensor(
                out=xn, in0=hn, scalar=st[("rho", t)][:, 1:2], in1=xn, op0=ALU.mult, op1=ALU.add
            )

        def cand_act(t):
            xn = st[("v", t)][:, 2 * H : 3 * H]
            nc.scalar.activation(
                out=xn, in_=xn, func=ACT.Tanh, scale=st[("rstd", t)][:, 2:3], bias=st[("mr", t)][:, 2:3]
            )

        def blend_gpsimd(t):
            v = st[("v", t)]
            d = v[:, 3 * H : 4 * H]
            nc.gpsimd.tensor_tensor(out=d, in0=v[:, 2 * H : 3 * H], in1=h_sb[:, t, :], op=ALU.subtract)
            nc.gpsimd.tensor_tensor(out=d, in0=d, in1=v[:, H : 2 * H], op=ALU.mult)

        def blend_out(t):
            v = st[("v", t)]
            po = ps_d.tile([P, H], F32, tag="d")
            nc.tensor.matmul(out=po[:], lhsT=ident[:], rhs=v[:, 2 * H : 3 * H], start=True, stop=False)
            nc.tensor.matmul(out=po[:], lhsT=neg_ident[:], rhs=v[:, 3 * H : 4 * H], start=False, stop=True)
            st[("po", t)] = po

        def store(t):
            res = results.tile([P, H], F32, tag="res", name="res")
            nc.scalar.copy(out=res[:], in_=st[("po", t)][:])
            nc.sync.dma_start(out=out_v[:, t, :], in_=res[:])

        def blend_vector(t):
            v = st[("v", t)]
            d = v[:, 3 * H : 4 * H]
            res = results.tile([P, H], F32, tag="res", name="res")
            nc.vector.tensor_tensor(out=d, in0=v[:, 2 * H : 3 * H], in1=h_sb[:, t, :], op=ALU.subtract)
            nc.vector.tensor_tensor(out=d, in0=d, in1=v[:, H : 2 * H], op=ALU.mult)
            nc.vector.tensor_tensor(out=res[:], in0=v[:, 2 * H : 3 * H], in1=d, op=ALU.subtract)
            nc.sync.dma_start(out=out_v[:, t, :], in_=res[:])

        def live(t):
            return 0 <= t < NT

        def at(t, fn, *args):
            if live(t):
                fn(t, *args)

        def on_gpsimd(t):
            return t < NT - LAST_ON_VECTOR

        with tc.manual_schedule():
            transposes(0)
            group(0)
            for j in range(3):
                spread_bias(j)
            quantise(0)
            transposes(1)
            group(1)
            for j in range(6):
                project(0, j)
                if j < 3:
                    spread_bias(j + 3)
            quantise(1)
            transposes(2)
            for i in range(0, NT + OE + 2):
                at(i - 1, rstds)
                if on_gpsimd(i - OE):
                    at(i - OE, blend_gpsimd)
                else:
                    at(i - OE, blend_vector)
                at(i, add_bias, 0)
                at(i + 1, project, 0)
                at(i, add_bias, 1)
                at(i + 1, project, 1)
                at(i, gate_sum, 0)
                at(i + 2, group)
                at(i, add_bias, 2)
                at(i + 1, project, 2)
                at(i, square, 0, 0, 2 * H)
                at(i, add_bias, 3)
                at(i + 1, project, 3)
                at(i, gate_sum, 1)
                at(i, add_bias, 4)
                at(i + 1, project, 4)
                at(i, square, 2, 2 * H, H)
                at(i, square, 1, 3 * H, 2 * H)
                at(i, add_bias, 5)
                at(i + 1, project, 5)
                at(i + 3, transposes)
                at(i, square, 3, 5 * H, H)
                if on_gpsimd(i - OE - 1):
                    at(i - OE - 1, store)
                at(i, var_eps, 0)
                at(i, var_eps, 1)
                at(i - OG, rs_sd)
                at(i - OG, rs_nm)
                at(i - OC, cand_reset)
                at(i - OG, rs_rho)
                at(i - OG, rs_mr)
                at(i + 2, quantise)
                at(i - OC, cand_sum)
                at(i - OG, rs_cg)
                at(i - OC, cand_act)
                if i - OG == NT - 1:
                    for lo in (0, H):
                        gates_sum(NT - 1, lo, lo + H)
                        gates_act(NT - 1, lo, lo + H)
                else:
                    at(i - OG, gates_sum)
                    at(i - OG, gates_act)
                if on_gpsimd(i - OE):
                    at(i - OE, blend_out)
